import numpy as np
import ml_dtypes


def mxq(x, axis, fmt="e4m3"):
    dtype, down = {"e4m3": (ml_dtypes.float8_e4m3fn, 7), "e5m2": (ml_dtypes.float8_e5m2, 14)}[fmt]
    v = np.moveaxis(np.asarray(x, np.float32).astype(ml_dtypes.bfloat16).astype(np.float64), axis, -1)
    blocks = v.reshape(v.shape[:-1] + (-1, 32))
    amax = np.abs(blocks).max(-1, keepdims=True)
    byte = np.maximum(np.where(amax > 0, np.frexp(amax)[1] - 1 + 127, 0) - down, 1)
    scale = np.exp2(byte - 127.0)
    codes = (blocks / scale).astype(np.float32).astype(dtype).astype(np.float64)
    return np.moveaxis((codes * scale).reshape(v.shape), -1, axis)


WIDE = False


def mx_kscale(k):
    if not WIDE:
        return np.ones(k)
    levels = np.array([10, -10, 5, -5, 0])
    a = np.random.permutation(np.resize(levels, k // 512 * 4)).reshape(k // 512, 4)
    idx = np.arange(k)
    return np.exp2(a[idx // 512, idx % 128 // 32])


BF16 = ml_dtypes.bfloat16


def bf(x):
    return np.asarray(x, np.float32).astype(BF16)


def f64(x):
    return np.asarray(x).astype(np.float64)


E2M1 = np.array([0.0, 0.5, 1.0, 1.5, 2.0, 3.0, 4.0, 6.0, -0.0, -0.5, -1.0, -1.5, -2.0, -3.0, -4.0, -6.0])


def pack_weight(w, fmt):
    k, n = w.shape
    w = f64(bf(w)).reshape(k // 32, 32, n)
    amax = np.abs(w).max(1)
    if fmt == "e4m3":
        byte = np.frexp(amax)[1] - 1 + 127 - 7
    else:
        mant, ex = np.frexp(amax / 6.0)
        byte = np.where(mant > 0.5, ex, ex - 1) + 127
    byte = np.clip(np.where(amax > 0, byte, 1), 1, 254)
    scaled = (w * np.exp2(127.0 - byte)[:, None, :]).reshape(k, n).astype(np.float32)
    by_word = np.ascontiguousarray(scaled.reshape(k // 512, 128, 4, n).transpose(0, 1, 3, 2))
    if fmt == "e4m3":
        words = by_word.astype(ml_dtypes.float8_e4m3fn).view(np.uint8)
    else:
        c = by_word.astype(ml_dtypes.float4_e2m1fn).view(np.uint8) & 0xF
        words = c[..., 0::2] | (c[..., 1::2] << 4)
    return np.ascontiguousarray(words), np.ascontiguousarray(byte.astype(np.uint8).reshape(k // 512, 16, n))


def unpack_weight(words, scales, fmt):
    g, p, n, _ = words.shape
    if fmt == "e4m3":
        vals = np.ascontiguousarray(words).view(ml_dtypes.float8_e4m3fn).astype(np.float64)
    else:
        nib = np.empty((g, p, n, 4), np.uint8)
        nib[..., 0::2] = words & 0xF
        nib[..., 1::2] = words >> 4
        vals = E2M1[nib]
    vals = vals * np.repeat(np.exp2(scales.astype(np.float64) - 127.0), 8, axis=1)[..., None]
    return vals.transpose(0, 1, 3, 2).reshape(g * 512, n)


N, IN_DIM, HID, OUT_DIM = 1024, 1024, 512, 256
CAT = 3 * HID


def log_softmax(v):
    d = v - v.max(-1, keepdims=True)
    return d - np.log(np.exp(d).sum(-1, keepdims=True))


def setup_inputs():
    s, t = mx_kscale(HID), mx_kscale(CAT)
    ta, tb, tc = t[:HID], t[HID:2 * HID], t[2 * HID:]
    u1 = bf(np.maximum(np.random.standard_normal((N, HID)) * 2.0, 0.0) * s)
    W2_1_words, W2_1_scales = pack_weight(np.random.standard_normal((HID, HID)) * 0.5 / np.sqrt(HID) / s[:, None] * tc, "e4m3")
    b2_1 = bf(np.random.standard_normal(HID) * 0.3 * tc)
    h = bf(np.random.standard_normal((N, HID)) * ta)
    h1 = bf(np.random.standard_normal((N, HID)) * 0.8 * tb)
    W_out_words, W_out_scales = pack_weight(np.random.standard_normal((CAT, OUT_DIM)) * 2.0 / np.sqrt(CAT) / t[:, None], "e4m3")
    b_out = bf(np.random.standard_normal(OUT_DIM) * 0.3)
    return {"u1": u1,
            "W2_1_words": W2_1_words,
            "W2_1_scales": W2_1_scales,
            "b2_1": b2_1,
            "h": h,
            "h1": h1,
            "W_out_words": W_out_words,
            "W_out_scales": W_out_scales,
            "b_out": b_out}


def reference(u1, W2_1_words, W2_1_scales, b2_1, h, h1, W_out_words, W_out_scales, b_out):
    h2 = (mxq(f64(u1), 1, "e4m3") @ unpack_weight(W2_1_words, W2_1_scales, "e4m3")) + f64(b2_1)
    cat = np.concatenate([f64(h), f64(h1), h2], axis=-1)
    logits = (mxq(cat, 1, "e4m3") @ unpack_weight(W_out_words, W_out_scales, "e4m3")) + f64(b_out)
    return log_softmax(logits)

@@ -1,0 +1,296 @@
+from contextlib import ExitStack
+
+import concourse.mybir as mybir
+from concourse.masks import make_identity
+
+F32 = mybir.dt.float32
+BF16 = mybir.dt.bfloat16
+I32 = mybir.dt.int32
+U32 = mybir.dt.uint32
+U8 = mybir.dt.uint8
+FP8X4 = mybir.dt.float8_e4m3fn_x4
+ALU = mybir.AluOpType
+ACT = mybir.ActivationFunctionType
+AXIS = mybir.AxisListType
+
+P = 128
+PACK = 4
+HALVES = 2
+NODES = 1024
+HID = 512
+CLASSES = 256
+GROUPS = 3
+TILES = NODES // P
+PAIR = 2
+ROUNDS = TILES // PAIR
+QUADRANTS = 4
+PAIR_NODES = PAIR * P
+
+FLOPS = 2 * NODES * HID * HID + 2 * NODES * GROUPS * HID * CLASSES
+
+
+def tile_gin_pc_kernel(
+    tc, u1, W2_1_words, W2_1_scales, b2_1, h, h1, W_out_words, W_out_scales, b_out, out
+):
+    nc = tc.nc
+    with ExitStack() as ctx:
+        const = ctx.enter_context(tc.tile_pool(name="const", bufs=1))
+        per_round = ctx.enter_context(tc.tile_pool(name="per_round", bufs=ROUNDS))
+        per_tile = ctx.enter_context(tc.tile_pool(name="per_tile", bufs=TILES))
+        scratch = ctx.enter_context(tc.tile_pool(name="scratch", bufs=2))
+        word_banks = ctx.enter_context(tc.psum_pool(name="word_banks", bufs=4))
+        h2_banks = ctx.enter_context(tc.psum_pool(name="h2_banks", bufs=2))
+        h2t_banks = ctx.enter_context(tc.psum_pool(name="h2t_banks", bufs=1))
+        logit_banks = ctx.enter_context(tc.psum_pool(name="logit_banks", bufs=1))
+        ctx.enter_context(tc.manual_schedule())
+
+        w21_plane = const.tile([P, HID], U8, align_bytes=64)
+        nc.vector.memset(w21_plane[:].bitcast(I32), 0)
+        bias_rows = const.tile([P, HID + CLASSES], BF16)
+        nc.vector.memset(bias_rows[:], 0.0)
+        ones = const.tile([P, P], BF16)
+        nc.vector.memset(ones[:], 1.0)
+        wout_planes = const.tile([P, CLASSES], U8, align_bytes=64)
+        nc.vector.memset(wout_planes[:].bitcast(I32), 0)
+        zero_col = const.tile([P, 1], F32)
+        nc.vector.memset(zero_col[:], 0.0)
+
+        one_col = const.tile([P, 1], F32)
+        nc.scalar.activation(out=one_col[:], in_=zero_col[:], func=ACT.Exp)
+
+        ident_f32 = const.tile([P, P], F32)
+        make_identity(nc, ident_f32[:])
+        ident_bf16 = const.tile([P, P], BF16)
+        make_identity(nc, ident_bf16[:])
+
+        def load_pair(x, r, tag):
+            x_sb = per_round.tile([P, PAIR, HID], BF16, tag=tag)
+            by_tile = x.rearrange("(p a) k -> p a k", a=TILES)
+            nc.sync.dma_start(out=x_sb[:], in_=by_tile[:, PAIR * r : PAIR * (r + 1), :])
+            return x_sb
+
+        u1_sb, h_sb, h1_sb = {}, {}, {}
+        u1_sb[0] = load_pair(u1, 0, "u1_sb")
+
+        nc.sync.dma_start(out=bias_rows[0:1, 0:HID], in_=b2_1.rearrange("(o n) -> o n", o=1))
+        nc.sync.dma_start(out=bias_rows[0:1, HID:], in_=b_out.rearrange("(o n) -> o n", o=1))
+
+        for quad in range(QUADRANTS):
+            nc.sync.dma_start(
+                out=w21_plane[32 * quad : 32 * quad + PACK, :].bitcast(I32),
+                in_=W2_1_scales[0, PACK * quad : PACK * (quad + 1), :].bitcast(I32),
+            )
+        w21_words = const.tile([P, HID], U32, align_bytes=64)
+        nc.sync.dma_start(
+            out=w21_words[:].bitcast(I32),
+            in_=W2_1_words[0].rearrange("p n t -> p (n t)").bitcast(I32),
+        )
+
+        u1_sb[1] = load_pair(u1, 1, "u1_sb")
+        h_sb[0] = load_pair(h, 0, "h_sb")
+        h1_sb[0] = load_pair(h1, 0, "h1_sb")
+        u1_sb[2] = load_pair(u1, 2, "u1_sb")
+        h_sb[1] = load_pair(h, 1, "h_sb")
+        h1_sb[1] = load_pair(h1, 1, "h1_sb")
+        u1_sb[3] = load_pair(u1, 3, "u1_sb")
+
+        for quad in range(QUADRANTS):
+            nc.sync.dma_start(
+                out=wout_planes[32 * quad : 32 * quad + PACK * GROUPS, :].bitcast(I32),
+                in_=W_out_scales[:, PACK * quad : PACK * (quad + 1), :].bitcast(I32),
+            )
+        wout_words = const.tile([P, GROUPS, CLASSES], U32, align_bytes=64)
+        nc.sync.dma_start(
+            out=wout_words[:].bitcast(I32),
+            in_=W_out_words.rearrange("g p n t -> p g (n t)").bitcast(I32),
+        )
+        for r in range(2, ROUNDS):
+            h_sb[r] = load_pair(h, r, "h_sb")
+            h1_sb[r] = load_pair(h1, r, "h1_sb")
+
+        def transpose_words(x_sb, grouped_cols):
+            words_t = word_banks.tile([P, PAIR, HALVES, P], F32)
+            for a in range(PAIR):
+                words = x_sb[:, a, :].bitcast(F32)
+                for u in range(HALVES):
+                    nc.tensor.transpose(
+                        words_t[:, a, u, :], words[:, u : HID // 2 : HALVES], ident_f32[:]
+                    )
+            nc.scalar.copy(
+                out=grouped_cols.bitcast(F32).rearrange(
+                    "p (a w u) -> p a w u", a=PAIR, u=HALVES
+                ),
+                in_=words_t[:].rearrange("p a u w -> p a w u"),
+            )
+
+        u1_codes, u1_planes = {}, {}
+
+        def prepare_u1(r):
+            u1_grouped = per_round.tile([P, PAIR_NODES * PACK], BF16, align_bytes=64)
+            transpose_words(u1_sb[r], u1_grouped[:])
+            u1_codes[r] = per_round.tile([P, PAIR_NODES], U32, align_bytes=64, name="u1_codes", tag="u1_codes")
+            u1_planes[r] = per_round.tile([P, PAIR_NODES], U8, align_bytes=64, name="u1_planes", tag="u1_planes")
+            nc.vector.quantize_mx(
+                out=u1_codes[r][:].bitcast(FP8X4), scales=u1_planes[r][:], in_=u1_grouped[:]
+            )
+
+        cat_codes, cat_planes = {}, {}
+
+        def prepare_h_h1(r):
+            hh_grouped = per_round.tile([P, 2, PAIR_NODES * PACK], BF16, align_bytes=64)
+            transpose_words(h_sb[r], hh_grouped[:, 0, :])
+            transpose_words(h1_sb[r], hh_grouped[:, 1, :])
+            cat_codes[r] = per_round.tile(
+                [P, GROUPS, PAIR_NODES], U32, align_bytes=64, name="cat_codes", tag="cat_codes"
+            )
+            cat_planes[r] = per_round.tile(
+                [P, GROUPS, PAIR_NODES], U8, align_bytes=64, name="cat_planes", tag="cat_planes"
+            )
+            nc.vector.quantize_mx(
+                out=cat_codes[r][:, 0:2, :].rearrange("p g w -> p (g w)").bitcast(FP8X4),
+                scales=cat_planes[r][:, 0:2, :].rearrange("p g w -> p (g w)"),
+                in_=hh_grouped[:].rearrange("p g c -> p (g c)"),
+            )
+
+        h2_sorted = {}
+
+        def first_matmul(r):
+            for a in range(PAIR):
+                nodes = slice(a * P, (a + 1) * P)
+                h2_acc = h2_banks.tile([P, HID], F32, tag="h2_bank")
+                nc.tensor.matmul_mx(
+                    out=h2_acc[:],
+                    lhsT=u1_codes[r][:, nodes].bitcast(FP8X4),
+                    lhsT_scale=u1_planes[r][:, nodes],
+                    rhs=w21_words[:].bitcast(FP8X4),
+                    rhs_scale=w21_plane[:],
+                    start=True,
+                    stop=True,
+                )
+                h2_sorted[r, a] = per_tile.tile([P, PACK, P], BF16, name="h2_sorted", tag="h2_sorted")
+                nc.vector.tensor_tensor(
+                    out=h2_sorted[r, a][:],
+                    in0=h2_acc[:].rearrange("p (j t) -> p t j", t=PACK),
+                    in1=b2_sorted[:],
+                    op=ALU.add,
+                )
+
+        h2_grouped = {}
+
+        def transpose_h2(r):
+            h2_t = h2t_banks.tile([P, PAIR, PACK, P], BF16)
+            for a in range(PAIR):
+                for t in range(PACK):
+                    nc.tensor.transpose(h2_t[:, a, t, :], h2_sorted[r, a][:, t, :], ident_bf16[:])
+            h2_grouped[r] = per_round.tile(
+                [P, PAIR_NODES * PACK], BF16, align_bytes=64, name="h2_grouped", tag="h2_grouped"
+            )
+            nc.scalar.copy(
+                out=h2_grouped[r][:].rearrange("p (a w t) -> p a w t", a=PAIR, t=PACK),
+                in_=h2_t[:].rearrange("p a t w -> p a w t"),
+            )
+
+        def quantise_h2(r):
+            nc.vector.quantize_mx(
+                out=cat_codes[r][:, 2, :].bitcast(FP8X4),
+                scales=cat_planes[r][:, 2, :],
+                in_=h2_grouped[r][:],
+            )
+
+        logits = {}
+        neg_max = const.tile([P, TILES], F32)
+        sums = const.tile([P, TILES], F32)
+
+        def second_matmul(r):
+            logit_acc = logit_banks.tile([P, PAIR, CLASSES], F32)
+            for a in range(PAIR):
+                nodes = slice(a * P, (a + 1) * P)
+                for g in range(GROUPS):
+                    nc.tensor.matmul_mx(
+                        out=logit_acc[:, a, :],
+                        lhsT=cat_codes[r][:, g, nodes].bitcast(FP8X4),
+                        lhsT_scale=cat_planes[r][:, g, nodes],
+                        rhs=wout_words[:, g, :].bitcast(FP8X4),
+                        rhs_scale=wout_planes[PACK * g : P, :],
+                        start=(g == 0),
+                        stop=(g == GROUPS - 1),
+                    )
+            logits[r] = per_round.tile([P, PAIR, CLASSES], F32, name="logits", tag="logits")
+            nc.vector.tensor_tensor(
+                out=logits[r][:],
+                in0=logit_acc[:],
+                in1=bout_all[:].unsqueeze(1).to_broadcast([P, PAIR, CLASSES]),
+                op=ALU.add,
+            )
+            nc.vector.tensor_reduce(
+                out=neg_max[:, PAIR * r : PAIR * (r + 1)],
+                in_=logits[r][:],
+                axis=AXIS.X,
+                op=ALU.max,
+                negate=True,
+            )
+
+        def exp_sums(r):
+            for a in range(PAIR):
+                i = PAIR * r + a
+                exps = scratch.tile([P, CLASSES], F32)
+                nc.scalar.activation(
+                    out=exps[:],
+                    in_=logits[r][:, a, :],
+                    func=ACT.Exp,
+                    bias=neg_max[:, i : i + 1],
+                    scale=1.0,
+                    accum_out=sums[:, i : i + 1],
+                )
+
+        prepare_u1(0)
+
+        b2_bank = h2_banks.tile([P, HID], F32, tag="h2_bank")
+        nc.tensor.matmul(out=b2_bank[:], lhsT=ones[:], rhs=bias_rows[:, 0:HID], start=True, stop=True)
+        b2_sorted = const.tile([P, PACK, P], F32)
+        nc.vector.tensor_copy(out=b2_sorted[:], in_=b2_bank[:].rearrange("p (j t) -> p t j", t=PACK))
+        bout_bank = h2_banks.tile([P, HID], F32, tag="h2_bank")
+        nc.tensor.matmul(
+            out=bout_bank[:, 0:CLASSES], lhsT=ones[:], rhs=bias_rows[:, HID:], start=True, stop=True
+        )
+        bout_all = const.tile([P, CLASSES], F32)
+        nc.vector.tensor_copy(out=bout_all[:], in_=bout_bank[:, 0:CLASSES])
+
+        for i in range(ROUNDS + 3):
+            if i + 1 < ROUNDS:
+                prepare_u1(i + 1)
+            if i < ROUNDS:
+                prepare_h_h1(i)
+            if 0 <= i - 3 < ROUNDS:
+                exp_sums(i - 3)
+            if 0 <= i - 1 < ROUNDS:
+                transpose_h2(i - 1)
+            if i < ROUNDS:
+                first_matmul(i)
+            if 0 <= i - 1 < ROUNDS:
+                quantise_h2(i - 1)
+            if 0 <= i - 2 < ROUNDS:
+                second_matmul(i - 2)
+
+        log_sums = const.tile([P, TILES], F32)
+        nc.scalar.activation(out=log_sums[:], in_=sums[:], func=ACT.Ln)
+        shift = const.tile([P, TILES], F32)
+        nc.vector.tensor_tensor(out=shift[:], in0=neg_max[:], in1=log_sums[:], op=ALU.subtract)
+        out_by_tile = out.rearrange("(p a) c -> p a c", a=TILES)
+        for r in range(ROUNDS):
+            first, second = PAIR * r, PAIR * r + 1
+            nc.vector.tensor_scalar(
+                out=logits[r][:, 0, :],
+                in0=logits[r][:, 0, :],
+                scalar1=shift[:, first : first + 1],
+                scalar2=None,
+                op0=ALU.add,
+            )
+            nc.scalar.activation(
+                out=logits[r][:, 1, :],
+                in_=logits[r][:, 1, :],
+                func=ACT.Identity,
+                bias=shift[:, second : second + 1],
+                scale=1.0,
+            )
+            nc.sync.dma_start(out=out_by_tile[:, PAIR * r : PAIR * (r + 1), :], in_=logits[r][:])

@@ -15,7 +15,8 @@ AXIS = mybir.AxisListType
 
 P = 128
 PACK = 4
-HALVES = 2
+PER_WORD = 2
+HALVES = PACK // PER_WORD
 NODES = 1024
 HID = 512
 CLASSES = 256
@@ -40,8 +41,7 @@ def tile_gin_pc_kernel(
         scratch = ctx.enter_context(tc.tile_pool(name="scratch", bufs=2))
         word_banks = ctx.enter_context(tc.psum_pool(name="word_banks", bufs=4))
         h2_banks = ctx.enter_context(tc.psum_pool(name="h2_banks", bufs=2))
-        h2t_banks = ctx.enter_context(tc.psum_pool(name="h2t_banks", bufs=1))
-        logit_banks = ctx.enter_context(tc.psum_pool(name="logit_banks", bufs=1))
+        logit_banks = ctx.enter_context(tc.psum_pool(name="logit_banks", bufs=2))
         ctx.enter_context(tc.manual_schedule())
 
         w21_plane = const.tile([P, HID], U8, align_bytes=64)
@@ -60,8 +60,6 @@ def tile_gin_pc_kernel(
 
         ident_f32 = const.tile([P, P], F32)
         make_identity(nc, ident_f32[:])
-        ident_bf16 = const.tile([P, P], BF16)
-        make_identity(nc, ident_bf16[:])
 
         def load_pair(x, r, tag):
             x_sb = per_round.tile([P, PAIR, HID], BF16, tag=tag)
@@ -86,13 +84,11 @@ def tile_gin_pc_kernel(
             in_=W2_1_words[0].rearrange("p n t -> p (n t)").bitcast(I32),
         )
 
-        u1_sb[1] = load_pair(u1, 1, "u1_sb")
-        h_sb[0] = load_pair(h, 0, "h_sb")
-        h1_sb[0] = load_pair(h1, 0, "h1_sb")
-        u1_sb[2] = load_pair(u1, 2, "u1_sb")
-        h_sb[1] = load_pair(h, 1, "h_sb")
-        h1_sb[1] = load_pair(h1, 1, "h1_sb")
-        u1_sb[3] = load_pair(u1, 3, "u1_sb")
+        for r in range(1, ROUNDS):
+            u1_sb[r] = load_pair(u1, r, "u1_sb")
+        for r in range(0, 2):
+            h_sb[r] = load_pair(h, r, "h_sb")
+            h1_sb[r] = load_pair(h1, r, "h1_sb")
 
         for quad in range(QUADRANTS):
             nc.sync.dma_start(
@@ -108,14 +104,11 @@ def tile_gin_pc_kernel(
             h_sb[r] = load_pair(h, r, "h_sb")
             h1_sb[r] = load_pair(h1, r, "h1_sb")
 
-        def transpose_words(x_sb, grouped_cols):
+        def transpose_words(word_cols, grouped_cols):
             words_t = word_banks.tile([P, PAIR, HALVES, P], F32)
             for a in range(PAIR):
-                words = x_sb[:, a, :].bitcast(F32)
                 for u in range(HALVES):
-                    nc.tensor.transpose(
-                        words_t[:, a, u, :], words[:, u : HID // 2 : HALVES], ident_f32[:]
-                    )
+                    nc.tensor.transpose(words_t[:, a, u, :], word_cols(a, u), ident_f32[:])
             nc.scalar.copy(
                 out=grouped_cols.bitcast(F32).rearrange(
                     "p (a w u) -> p a w u", a=PAIR, u=HALVES
@@ -123,35 +116,52 @@ def tile_gin_pc_kernel(
                 in_=words_t[:].rearrange("p a u w -> p a w u"),
             )
 
-        u1_codes, u1_planes = {}, {}
+        def input_words(x_sb):
+            return lambda a, u: x_sb[:, a, :].bitcast(F32)[:, u : HID // PER_WORD : HALVES]
 
-        def prepare_u1(r):
-            u1_grouped = per_round.tile([P, PAIR_NODES * PACK], BF16, align_bytes=64)
-            transpose_words(u1_sb[r], u1_grouped[:])
-            u1_codes[r] = per_round.tile([P, PAIR_NODES], U32, align_bytes=64, name="u1_codes", tag="u1_codes")
-            u1_planes[r] = per_round.tile([P, PAIR_NODES], U8, align_bytes=64, name="u1_planes", tag="u1_planes")
-            nc.vector.quantize_mx(
-                out=u1_codes[r][:].bitcast(FP8X4), scales=u1_planes[r][:], in_=u1_grouped[:]
+        u1_grouped, u1_codes, u1_planes = {}, {}, {}
+        cat_grouped, cat_codes, cat_planes = {}, {}, {}
+        for r in range(ROUNDS):
+            u1_grouped[r] = per_round.tile(
+                [P, PAIR_NODES * PACK], BF16, align_bytes=64, name="u1_grouped", tag="u1_grouped"
             )
-
-        cat_codes, cat_planes = {}, {}
-
-        def prepare_h_h1(r):
-            hh_grouped = per_round.tile([P, 2, PAIR_NODES * PACK], BF16, align_bytes=64)
-            transpose_words(h_sb[r], hh_grouped[:, 0, :])
-            transpose_words(h1_sb[r], hh_grouped[:, 1, :])
+            u1_codes[r] = per_round.tile(
+                [P, PAIR_NODES], U32, align_bytes=64, name="u1_codes", tag="u1_codes"
+            )
+            u1_planes[r] = per_round.tile(
+                [P, PAIR_NODES], U8, align_bytes=64, name="u1_planes", tag="u1_planes"
+            )
+            cat_grouped[r] = per_round.tile(
+                [P, GROUPS, PAIR_NODES * PACK], BF16, align_bytes=64,
+                name="cat_grouped", tag="cat_grouped",
+            )
             cat_codes[r] = per_round.tile(
                 [P, GROUPS, PAIR_NODES], U32, align_bytes=64, name="cat_codes", tag="cat_codes"
             )
             cat_planes[r] = per_round.tile(
                 [P, GROUPS, PAIR_NODES], U8, align_bytes=64, name="cat_planes", tag="cat_planes"
             )
+
+        def transpose_u1(r):
+            transpose_words(input_words(u1_sb[r]), u1_grouped[r][:])
+
+        def quantise_u1(r):
+            nc.vector.quantize_mx(
+                out=u1_codes[r][:].bitcast(FP8X4), scales=u1_planes[r][:], in_=u1_grouped[r][:]
+            )
+
+        def transpose_h_h1(r):
+            transpose_words(input_words(h_sb[r]), cat_grouped[r][:, 0, :])
+            transpose_words(input_words(h1_sb[r]), cat_grouped[r][:, 1, :])
+
+        def quantise_h_h1(r):
             nc.vector.quantize_mx(
                 out=cat_codes[r][:, 0:2, :].rearrange("p g w -> p (g w)").bitcast(FP8X4),
                 scales=cat_planes[r][:, 0:2, :].rearrange("p g w -> p (g w)"),
-                in_=hh_grouped[:].rearrange("p g c -> p (g c)"),
+                in_=cat_grouped[r][:, 0:2, :].rearrange("p g c -> p (g c)"),
             )
 
+        by_half = "p (j u e) -> p u j e"
         h2_sorted = {}
 
         def first_matmul(r):
@@ -167,47 +177,40 @@ def tile_gin_pc_kernel(
                     start=True,
                     stop=True,
                 )
-                h2_sorted[r, a] = per_tile.tile([P, PACK, P], BF16, name="h2_sorted", tag="h2_sorted")
+                h2_sorted[r, a] = per_tile.tile(
+                    [P, HALVES, P, PER_WORD], BF16, name="h2_sorted", tag="h2_sorted"
+                )
                 nc.vector.tensor_tensor(
                     out=h2_sorted[r, a][:],
-                    in0=h2_acc[:].rearrange("p (j t) -> p t j", t=PACK),
+                    in0=h2_acc[:].rearrange(by_half, u=HALVES, e=PER_WORD),
                     in1=b2_sorted[:],
                     op=ALU.add,
                 )
 
-        h2_grouped = {}
-
         def transpose_h2(r):
-            h2_t = h2t_banks.tile([P, PAIR, PACK, P], BF16)
-            for a in range(PAIR):
-                for t in range(PACK):
-                    nc.tensor.transpose(h2_t[:, a, t, :], h2_sorted[r, a][:, t, :], ident_bf16[:])
-            h2_grouped[r] = per_round.tile(
-                [P, PAIR_NODES * PACK], BF16, align_bytes=64, name="h2_grouped", tag="h2_grouped"
-            )
-            nc.scalar.copy(
-                out=h2_grouped[r][:].rearrange("p (a w t) -> p a w t", a=PAIR, t=PACK),
-                in_=h2_t[:].rearrange("p a t w -> p a w t"),
+            transpose_words(
+                lambda a, u: h2_sorted[r, a][:, u, :, :].rearrange("p j e -> p (j e)").bitcast(F32),
+                cat_grouped[r][:, 2, :],
             )
 
         def quantise_h2(r):
             nc.vector.quantize_mx(
                 out=cat_codes[r][:, 2, :].bitcast(FP8X4),
                 scales=cat_planes[r][:, 2, :],
-                in_=h2_grouped[r][:],
+                in_=cat_grouped[r][:, 2, :],
             )
 
-        logits = {}
+        logit_acc, logits = {}, {}
         neg_max = const.tile([P, TILES], F32)
         sums = const.tile([P, TILES], F32)
 
         def second_matmul(r):
-            logit_acc = logit_banks.tile([P, PAIR, CLASSES], F32)
+            logit_acc[r] = logit_banks.tile([P, PAIR, CLASSES], F32, name="logit_acc", tag="logit_acc")
             for a in range(PAIR):
                 nodes = slice(a * P, (a + 1) * P)
                 for g in range(GROUPS):
                     nc.tensor.matmul_mx(
-                        out=logit_acc[:, a, :],
+                        out=logit_acc[r][:, a, :],
                         lhsT=cat_codes[r][:, g, nodes].bitcast(FP8X4),
                         lhsT_scale=cat_planes[r][:, g, nodes],
                         rhs=wout_words[:, g, :].bitcast(FP8X4),
@@ -215,10 +218,12 @@ def tile_gin_pc_kernel(
                         start=(g == 0),
                         stop=(g == GROUPS - 1),
                     )
+
+        def logits_and_max(r):
             logits[r] = per_round.tile([P, PAIR, CLASSES], F32, name="logits", tag="logits")
             nc.vector.tensor_tensor(
                 out=logits[r][:],
-                in0=logit_acc[:],
+                in0=logit_acc[r][:],
                 in1=bout_all[:].unsqueeze(1).to_broadcast([P, PAIR, CLASSES]),
                 op=ALU.add,
             )
@@ -243,12 +248,13 @@ def tile_gin_pc_kernel(
                     accum_out=sums[:, i : i + 1],
                 )
 
-        prepare_u1(0)
+        transpose_u1(0)
+        quantise_u1(0)
 
         b2_bank = h2_banks.tile([P, HID], F32, tag="h2_bank")
         nc.tensor.matmul(out=b2_bank[:], lhsT=ones[:], rhs=bias_rows[:, 0:HID], start=True, stop=True)
-        b2_sorted = const.tile([P, PACK, P], F32)
-        nc.vector.tensor_copy(out=b2_sorted[:], in_=b2_bank[:].rearrange("p (j t) -> p t j", t=PACK))
+        b2_sorted = const.tile([P, HALVES, P, PER_WORD], F32)
+        nc.vector.tensor_copy(out=b2_sorted[:], in_=b2_bank[:].rearrange(by_half, u=HALVES, e=PER_WORD))
         bout_bank = h2_banks.tile([P, HID], F32, tag="h2_bank")
         nc.tensor.matmul(
             out=bout_bank[:, 0:CLASSES], lhsT=ones[:], rhs=bias_rows[:, HID:], start=True, stop=True
@@ -256,41 +262,37 @@ def tile_gin_pc_kernel(
         bout_all = const.tile([P, CLASSES], F32)
         nc.vector.tensor_copy(out=bout_all[:], in_=bout_bank[:, 0:CLASSES])
 
-        for i in range(ROUNDS + 3):
-            if i + 1 < ROUNDS:
-                prepare_u1(i + 1)
-            if i < ROUNDS:
-                prepare_h_h1(i)
-            if 0 <= i - 3 < ROUNDS:
-                exp_sums(i - 3)
-            if 0 <= i - 1 < ROUNDS:
-                transpose_h2(i - 1)
-            if i < ROUNDS:
-                first_matmul(i)
-            if 0 <= i - 1 < ROUNDS:
-                quantise_h2(i - 1)
-            if 0 <= i - 2 < ROUNDS:
-                second_matmul(i - 2)
+        transpose_u1(1)
+        quantise_u1(1)
+
+        def if_round(stage, r):
+            if 0 <= r < ROUNDS:
+                stage(r)
+
+        for i in range(ROUNDS + 4):
+            if_round(quantise_h2, i - 2)
+            if_round(transpose_u1, i + 2)
+            if_round(first_matmul, i)
+            if_round(quantise_u1, i + 2)
+            if_round(second_matmul, i - 3)
+            if_round(quantise_h_h1, i - 2)
+            if_round(logits_and_max, i - 3)
+            if_round(exp_sums, i - 4)
+            if_round(transpose_h2, i - 1)
+            if_round(transpose_h_h1, i - 1)
 
         log_sums = const.tile([P, TILES], F32)
         nc.scalar.activation(out=log_sums[:], in_=sums[:], func=ACT.Ln)
-        shift = const.tile([P, TILES], F32)
-        nc.vector.tensor_tensor(out=shift[:], in0=neg_max[:], in1=log_sums[:], op=ALU.subtract)
         out_by_tile = out.rearrange("(p a) c -> p a c", a=TILES)
         for r in range(ROUNDS):
-            first, second = PAIR * r, PAIR * r + 1
-            nc.vector.tensor_scalar(
-                out=logits[r][:, 0, :],
-                in0=logits[r][:, 0, :],
-                scalar1=shift[:, first : first + 1],
-                scalar2=None,
-                op0=ALU.add,
-            )
-            nc.scalar.activation(
-                out=logits[r][:, 1, :],
-                in_=logits[r][:, 1, :],
-                func=ACT.Identity,
-                bias=shift[:, second : second + 1],
-                scale=1.0,
-            )
+            for a in range(PAIR):
+                i = PAIR * r + a
+                nc.vector.tensor_scalar(
+                    out=logits[r][:, a, :],
+                    in0=logits[r][:, a, :],
+                    scalar1=neg_max[:, i : i + 1],
+                    scalar2=log_sums[:, i : i + 1],
+                    op0=ALU.add,
+                    op1=ALU.subtract,
+                )
             nc.sync.dma_start(out=out_by_tile[:, PAIR * r : PAIR * (r + 1), :], in_=logits[r][:])

@@ -46,8 +46,8 @@ def tile_gin_pc_kernel(
 
         w21_plane = const.tile([P, HID], U8, align_bytes=64)
         nc.vector.memset(w21_plane[:].bitcast(I32), 0)
-        bias_rows = const.tile([P, HID + CLASSES], BF16)
-        nc.vector.memset(bias_rows[:], 0.0)
+        b2_rows = const.tile([P, HID], BF16)
+        nc.vector.memset(b2_rows[:], 0.0)
         ones = const.tile([P, P], BF16)
         nc.vector.memset(ones[:], 1.0)
         wout_planes = const.tile([P, CLASSES], U8, align_bytes=64)
@@ -70,9 +70,6 @@ def tile_gin_pc_kernel(
         u1_sb, h_sb, h1_sb = {}, {}, {}
         u1_sb[0] = load_pair(u1, 0, "u1_sb")
 
-        nc.sync.dma_start(out=bias_rows[0:1, 0:HID], in_=b2_1.rearrange("(o n) -> o n", o=1))
-        nc.sync.dma_start(out=bias_rows[0:1, HID:], in_=b_out.rearrange("(o n) -> o n", o=1))
-
         for quad in range(QUADRANTS):
             nc.sync.dma_start(
                 out=w21_plane[32 * quad : 32 * quad + PACK, :].bitcast(I32),
@@ -84,6 +81,7 @@ def tile_gin_pc_kernel(
             in_=W2_1_words[0].rearrange("p n t -> p (n t)").bitcast(I32),
         )
 
+        nc.sync.dma_start(out=b2_rows[0:1, :], in_=b2_1.rearrange("(o n) -> o n", o=1))
         for r in range(1, ROUNDS):
             u1_sb[r] = load_pair(u1, r, "u1_sb")
         for r in range(0, 2):
@@ -100,6 +98,8 @@ def tile_gin_pc_kernel(
             out=wout_words[:].bitcast(I32),
             in_=W_out_words.rearrange("g p n t -> p g (n t)").bitcast(I32),
         )
+        bout_all = const.tile([P, CLASSES], BF16)
+        nc.sync.dma_start(out=bout_all[:], in_=b_out.partition_broadcast(P))
         for r in range(2, ROUNDS):
             h_sb[r] = load_pair(h, r, "h_sb")
             h1_sb[r] = load_pair(h1, r, "h1_sb")
@@ -252,15 +252,9 @@ def tile_gin_pc_kernel(
         quantise_u1(0)
 
         b2_bank = h2_banks.tile([P, HID], F32, tag="h2_bank")
-        nc.tensor.matmul(out=b2_bank[:], lhsT=ones[:], rhs=bias_rows[:, 0:HID], start=True, stop=True)
+        nc.tensor.matmul(out=b2_bank[:], lhsT=ones[:], rhs=b2_rows[:], start=True, stop=True)
         b2_sorted = const.tile([P, HALVES, P, PER_WORD], F32)
         nc.vector.tensor_copy(out=b2_sorted[:], in_=b2_bank[:].rearrange(by_half, u=HALVES, e=PER_WORD))
-        bout_bank = h2_banks.tile([P, HID], F32, tag="h2_bank")
-        nc.tensor.matmul(
-            out=bout_bank[:, 0:CLASSES], lhsT=ones[:], rhs=bias_rows[:, HID:], start=True, stop=True
-        )
-        bout_all = const.tile([P, CLASSES], F32)
-        nc.vector.tensor_copy(out=bout_all[:], in_=bout_bank[:, 0:CLASSES])
 
         transpose_u1(1)
         quantise_u1(1)

@@ -22,10 +22,11 @@ HID = 512
 CLASSES = 256
 GROUPS = 3
 TILES = NODES // P
-PAIR = 2
-ROUNDS = TILES // PAIR
+ROUND_TILES = (1, 2, 2, 2, 1)
+ROUNDS = len(ROUND_TILES)
+FIRST_TILE = tuple(sum(ROUND_TILES[:r]) for r in range(ROUNDS))
 QUADRANTS = 4
-PAIR_NODES = PAIR * P
+assert sum(ROUND_TILES) == TILES
 
 FLOPS = 2 * NODES * HID * HID + 2 * NODES * GROUPS * HID * CLASSES
 
@@ -46,8 +47,8 @@ def tile_gin_pc_kernel(
 
         w21_plane = const.tile([P, HID], U8, align_bytes=64)
         nc.vector.memset(w21_plane[:].bitcast(I32), 0)
-        b2_rows = const.tile([P, HID], BF16)
-        nc.vector.memset(b2_rows[:], 0.0)
+        bias_rows = const.tile([P, HID + CLASSES], BF16)
+        nc.vector.memset(bias_rows[:], 0.0)
         ones = const.tile([P, P], BF16)
         nc.vector.memset(ones[:], 1.0)
         wout_planes = const.tile([P, CLASSES], U8, align_bytes=64)
@@ -61,14 +62,19 @@ def tile_gin_pc_kernel(
         ident_f32 = const.tile([P, P], F32)
         make_identity(nc, ident_f32[:])
 
-        def load_pair(x, r, tag):
-            x_sb = per_round.tile([P, PAIR, HID], BF16, tag=tag)
-            by_tile = x.rearrange("(p a) k -> p a k", a=TILES)
-            nc.sync.dma_start(out=x_sb[:], in_=by_tile[:, PAIR * r : PAIR * (r + 1), :])
+        def tiles_of(r):
+            return slice(FIRST_TILE[r], FIRST_TILE[r] + ROUND_TILES[r])
+
+        def load_round(x, r, tag):
+            x_sb = per_round.tile([P, ROUND_TILES[r], HID], BF16, tag=tag)
+            nc.sync.dma_start(
+                out=x_sb[:], in_=x.rearrange("(p a) k -> p a k", a=TILES)[:, tiles_of(r), :]
+            )
             return x_sb
 
         u1_sb, h_sb, h1_sb = {}, {}, {}
-        u1_sb[0] = load_pair(u1, 0, "u1_sb")
+        u1_sb[0] = load_round(u1, 0, "u1_sb")
+        u1_sb[1] = load_round(u1, 1, "u1_sb")
 
         for quad in range(QUADRANTS):
             nc.sync.dma_start(
@@ -81,12 +87,13 @@ def tile_gin_pc_kernel(
             in_=W2_1_words[0].rearrange("p n t -> p (n t)").bitcast(I32),
         )
 
-        nc.sync.dma_start(out=b2_rows[0:1, :], in_=b2_1.rearrange("(o n) -> o n", o=1))
-        for r in range(1, ROUNDS):
-            u1_sb[r] = load_pair(u1, r, "u1_sb")
+        nc.sync.dma_start(out=bias_rows[0:1, 0:HID], in_=b2_1.rearrange("(o n) -> o n", o=1))
+        for r in range(2, ROUNDS):
+            u1_sb[r] = load_round(u1, r, "u1_sb")
+        nc.sync.dma_start(out=bias_rows[0:1, HID:], in_=b_out.rearrange("(o n) -> o n", o=1))
         for r in range(0, 2):
-            h_sb[r] = load_pair(h, r, "h_sb")
-            h1_sb[r] = load_pair(h1, r, "h1_sb")
+            h_sb[r] = load_round(h, r, "h_sb")
+            h1_sb[r] = load_round(h1, r, "h1_sb")
 
         for quad in range(QUADRANTS):
             nc.sync.dma_start(
@@ -98,20 +105,18 @@ def tile_gin_pc_kernel(
             out=wout_words[:].bitcast(I32),
             in_=W_out_words.rearrange("g p n t -> p g (n t)").bitcast(I32),
         )
-        bout_all = const.tile([P, CLASSES], BF16)
-        nc.sync.dma_start(out=bout_all[:], in_=b_out.partition_broadcast(P))
         for r in range(2, ROUNDS):
-            h_sb[r] = load_pair(h, r, "h_sb")
-            h1_sb[r] = load_pair(h1, r, "h1_sb")
+            h_sb[r] = load_round(h, r, "h_sb")
+            h1_sb[r] = load_round(h1, r, "h1_sb")
 
-        def transpose_words(word_cols, grouped_cols):
-            words_t = word_banks.tile([P, PAIR, HALVES, P], F32)
-            for a in range(PAIR):
+        def transpose_words(r, word_cols, grouped_cols):
+            words_t = word_banks.tile([P, ROUND_TILES[r], HALVES, P], F32)
+            for a in range(ROUND_TILES[r]):
                 for u in range(HALVES):
                     nc.tensor.transpose(words_t[:, a, u, :], word_cols(a, u), ident_f32[:])
             nc.scalar.copy(
                 out=grouped_cols.bitcast(F32).rearrange(
-                    "p (a w u) -> p a w u", a=PAIR, u=HALVES
+                    "p (a w u) -> p a w u", a=ROUND_TILES[r], u=HALVES
                 ),
                 in_=words_t[:].rearrange("p a u w -> p a w u"),
             )
@@ -122,28 +127,29 @@ def tile_gin_pc_kernel(
         u1_grouped, u1_codes, u1_planes = {}, {}, {}
         cat_grouped, cat_codes, cat_planes = {}, {}, {}
         for r in range(ROUNDS):
+            nodes = ROUND_TILES[r] * P
             u1_grouped[r] = per_round.tile(
-                [P, PAIR_NODES * PACK], BF16, align_bytes=64, name="u1_grouped", tag="u1_grouped"
+                [P, nodes * PACK], BF16, align_bytes=64, name="u1_grouped", tag="u1_grouped"
             )
             u1_codes[r] = per_round.tile(
-                [P, PAIR_NODES], U32, align_bytes=64, name="u1_codes", tag="u1_codes"
+                [P, nodes], U32, align_bytes=64, name="u1_codes", tag="u1_codes"
             )
             u1_planes[r] = per_round.tile(
-                [P, PAIR_NODES], U8, align_bytes=64, name="u1_planes", tag="u1_planes"
+                [P, nodes], U8, align_bytes=64, name="u1_planes", tag="u1_planes"
             )
             cat_grouped[r] = per_round.tile(
-                [P, GROUPS, PAIR_NODES * PACK], BF16, align_bytes=64,
+                [P, GROUPS, nodes * PACK], BF16, align_bytes=64,
                 name="cat_grouped", tag="cat_grouped",
             )
             cat_codes[r] = per_round.tile(
-                [P, GROUPS, PAIR_NODES], U32, align_bytes=64, name="cat_codes", tag="cat_codes"
+                [P, GROUPS, nodes], U32, align_bytes=64, name="cat_codes", tag="cat_codes"
             )
             cat_planes[r] = per_round.tile(
-                [P, GROUPS, PAIR_NODES], U8, align_bytes=64, name="cat_planes", tag="cat_planes"
+                [P, GROUPS, nodes], U8, align_bytes=64, name="cat_planes", tag="cat_planes"
             )
 
         def transpose_u1(r):
-            transpose_words(input_words(u1_sb[r]), u1_grouped[r][:])
+            transpose_words(r, input_words(u1_sb[r]), u1_grouped[r][:])
 
         def quantise_u1(r):
             nc.vector.quantize_mx(
@@ -151,8 +157,8 @@ def tile_gin_pc_kernel(
             )
 
         def transpose_h_h1(r):
-            transpose_words(input_words(h_sb[r]), cat_grouped[r][:, 0, :])
-            transpose_words(input_words(h1_sb[r]), cat_grouped[r][:, 1, :])
+            transpose_words(r, input_words(h_sb[r]), cat_grouped[r][:, 0, :])
+            transpose_words(r, input_words(h1_sb[r]), cat_grouped[r][:, 1, :])
 
         def quantise_h_h1(r):
             nc.vector.quantize_mx(
@@ -165,13 +171,13 @@ def tile_gin_pc_kernel(
         h2_sorted = {}
 
         def first_matmul(r):
-            for a in range(PAIR):
-                nodes = slice(a * P, (a + 1) * P)
+            for a in range(ROUND_TILES[r]):
+                tile_nodes = slice(a * P, (a + 1) * P)
                 h2_acc = h2_banks.tile([P, HID], F32, tag="h2_bank")
                 nc.tensor.matmul_mx(
                     out=h2_acc[:],
-                    lhsT=u1_codes[r][:, nodes].bitcast(FP8X4),
-                    lhsT_scale=u1_planes[r][:, nodes],
+                    lhsT=u1_codes[r][:, tile_nodes].bitcast(FP8X4),
+                    lhsT_scale=u1_planes[r][:, tile_nodes],
                     rhs=w21_words[:].bitcast(FP8X4),
                     rhs_scale=w21_plane[:],
                     start=True,
@@ -189,6 +195,7 @@ def tile_gin_pc_kernel(
 
         def transpose_h2(r):
             transpose_words(
+                r,
                 lambda a, u: h2_sorted[r, a][:, u, :, :].rearrange("p j e -> p (j e)").bitcast(F32),
                 cat_grouped[r][:, 2, :],
             )
@@ -205,14 +212,16 @@ def tile_gin_pc_kernel(
         sums = const.tile([P, TILES], F32)
 
         def second_matmul(r):
-            logit_acc[r] = logit_banks.tile([P, PAIR, CLASSES], F32, name="logit_acc", tag="logit_acc")
-            for a in range(PAIR):
-                nodes = slice(a * P, (a + 1) * P)
+            logit_acc[r] = logit_banks.tile(
+                [P, ROUND_TILES[r], CLASSES], F32, name="logit_acc", tag="logit_acc"
+            )
+            for a in range(ROUND_TILES[r]):
+                tile_nodes = slice(a * P, (a + 1) * P)
                 for g in range(GROUPS):
                     nc.tensor.matmul_mx(
                         out=logit_acc[r][:, a, :],
-                        lhsT=cat_codes[r][:, g, nodes].bitcast(FP8X4),
-                        lhsT_scale=cat_planes[r][:, g, nodes],
+                        lhsT=cat_codes[r][:, g, tile_nodes].bitcast(FP8X4),
+                        lhsT_scale=cat_planes[r][:, g, tile_nodes],
                         rhs=wout_words[:, g, :].bitcast(FP8X4),
                         rhs_scale=wout_planes[PACK * g : P, :],
                         start=(g == 0),
@@ -220,24 +229,21 @@ def tile_gin_pc_kernel(
                     )
 
         def logits_and_max(r):
-            logits[r] = per_round.tile([P, PAIR, CLASSES], F32, name="logits", tag="logits")
+            shape = [P, ROUND_TILES[r], CLASSES]
+            logits[r] = per_round.tile(shape, F32, name="logits", tag="logits")
             nc.vector.tensor_tensor(
                 out=logits[r][:],
                 in0=logit_acc[r][:],
-                in1=bout_all[:].unsqueeze(1).to_broadcast([P, PAIR, CLASSES]),
+                in1=bout_all[:].unsqueeze(1).to_broadcast(shape),
                 op=ALU.add,
             )
             nc.vector.tensor_reduce(
-                out=neg_max[:, PAIR * r : PAIR * (r + 1)],
-                in_=logits[r][:],
-                axis=AXIS.X,
-                op=ALU.max,
-                negate=True,
+                out=neg_max[:, tiles_of(r)], in_=logits[r][:], axis=AXIS.X, op=ALU.max, negate=True
             )
 
         def exp_sums(r):
-            for a in range(PAIR):
-                i = PAIR * r + a
+            for a in range(ROUND_TILES[r]):
+                i = FIRST_TILE[r] + a
                 exps = scratch.tile([P, CLASSES], F32)
                 nc.scalar.activation(
                     out=exps[:],
@@ -252,7 +258,7 @@ def tile_gin_pc_kernel(
         quantise_u1(0)
 
         b2_bank = h2_banks.tile([P, HID], F32, tag="h2_bank")
-        nc.tensor.matmul(out=b2_bank[:], lhsT=ones[:], rhs=b2_rows[:], start=True, stop=True)
+        nc.tensor.matmul(out=b2_bank[:], lhsT=ones[:], rhs=bias_rows[:, 0:HID], start=True, stop=True)
         b2_sorted = const.tile([P, HALVES, P, PER_WORD], F32)
         nc.vector.tensor_copy(out=b2_sorted[:], in_=b2_bank[:].rearrange(by_half, u=HALVES, e=PER_WORD))
 
@@ -263,7 +269,7 @@ def tile_gin_pc_kernel(
             if 0 <= r < ROUNDS:
                 stage(r)
 
-        for i in range(ROUNDS + 4):
+        def step(i):
             if_round(quantise_h2, i - 2)
             if_round(transpose_u1, i + 2)
             if_round(first_matmul, i)
@@ -275,12 +281,21 @@ def tile_gin_pc_kernel(
             if_round(transpose_h2, i - 1)
             if_round(transpose_h_h1, i - 1)
 
+        step(0)
+        bout_bank = logit_banks.tile([P, CLASSES], F32, tag="logit_acc")
+        nc.tensor.matmul(
+            out=bout_bank[:], lhsT=ones[:], rhs=bias_rows[:, HID:], start=True, stop=True
+        )
+        bout_all = const.tile([P, CLASSES], F32)
+        nc.scalar.copy(out=bout_all[:], in_=bout_bank[:])
+        for i in range(1, ROUNDS + 4):
+            step(i)
+
         log_sums = const.tile([P, TILES], F32)
         nc.scalar.activation(out=log_sums[:], in_=sums[:], func=ACT.Ln)
-        out_by_tile = out.rearrange("(p a) c -> p a c", a=TILES)
         for r in range(ROUNDS):
-            for a in range(PAIR):
-                i = PAIR * r + a
+            for a in range(ROUND_TILES[r]):
+                i = FIRST_TILE[r] + a
                 nc.vector.tensor_scalar(
                     out=logits[r][:, a, :],
                     in0=logits[r][:, a, :],
@@ -289,4 +304,6 @@ def tile_gin_pc_kernel(
                     op0=ALU.add,
                     op1=ALU.subtract,
                 )
-            nc.sync.dma_start(out=out_by_tile[:, PAIR * r : PAIR * (r + 1), :], in_=logits[r][:])
+            nc.sync.dma_start(
+                out=out.rearrange("(p a) c -> p a c", a=TILES)[:, tiles_of(r), :], in_=logits[r][:]
+            )

@@ -45,10 +45,10 @@ def tile_gin_pc_kernel(
         logit_banks = ctx.enter_context(tc.psum_pool(name="logit_banks", bufs=2))
         ctx.enter_context(tc.manual_schedule())
 
-        w21_plane = const.tile([P, HID], U8, align_bytes=64)
-        nc.vector.memset(w21_plane[:].bitcast(I32), 0)
         bias_rows = const.tile([P, HID + CLASSES], BF16)
         nc.vector.memset(bias_rows[:], 0.0)
+        w21_plane = const.tile([P, HID], U8, align_bytes=64)
+        nc.vector.memset(w21_plane[:].bitcast(I32), 0)
         ones = const.tile([P, P], BF16)
         nc.vector.memset(ones[:], 1.0)
         wout_planes = const.tile([P, CLASSES], U8, align_bytes=64)
@@ -74,6 +74,7 @@ def tile_gin_pc_kernel(
 
         u1_sb, h_sb, h1_sb = {}, {}, {}
         u1_sb[0] = load_round(u1, 0, "u1_sb")
+        nc.sync.dma_start(out=bias_rows[0:1, 0:HID], in_=b2_1.rearrange("(o n) -> o n", o=1))
         u1_sb[1] = load_round(u1, 1, "u1_sb")
 
         for quad in range(QUADRANTS):
@@ -87,7 +88,6 @@ def tile_gin_pc_kernel(
             in_=W2_1_words[0].rearrange("p n t -> p (n t)").bitcast(I32),
         )
 
-        nc.sync.dma_start(out=bias_rows[0:1, 0:HID], in_=b2_1.rearrange("(o n) -> o n", o=1))
         for r in range(2, ROUNDS):
             u1_sb[r] = load_round(u1, r, "u1_sb")
         nc.sync.dma_start(out=bias_rows[0:1, HID:], in_=b_out.rearrange("(o n) -> o n", o=1))
@@ -271,10 +271,10 @@ def tile_gin_pc_kernel(
 
         def step(i):
             if_round(quantise_h2, i - 2)
-            if_round(transpose_u1, i + 2)
             if_round(first_matmul, i)
-            if_round(quantise_u1, i + 2)
             if_round(second_matmul, i - 3)
+            if_round(transpose_u1, i + 2)
+            if_round(quantise_u1, i + 2)
             if_round(quantise_h_h1, i - 2)
             if_round(logits_and_max, i - 3)
             if_round(exp_sums, i - 4)
@@ -282,13 +282,14 @@ def tile_gin_pc_kernel(
             if_round(transpose_h_h1, i - 1)
 
         step(0)
+        step(1)
         bout_bank = logit_banks.tile([P, CLASSES], F32, tag="logit_acc")
         nc.tensor.matmul(
             out=bout_bank[:], lhsT=ones[:], rhs=bias_rows[:, HID:], start=True, stop=True
         )
         bout_all = const.tile([P, CLASSES], F32)
         nc.scalar.copy(out=bout_all[:], in_=bout_bank[:])
-        for i in range(1, ROUNDS + 4):
+        for i in range(2, ROUNDS + 4):
             step(i)
 
         log_sums = const.tile([P, TILES], F32)

from contextlib import ExitStack

import concourse.mybir as mybir
from concourse.masks import make_identity

F32 = mybir.dt.float32
BF16 = mybir.dt.bfloat16
I32 = mybir.dt.int32
U32 = mybir.dt.uint32
U8 = mybir.dt.uint8
FP8X4 = mybir.dt.float8_e4m3fn_x4
ALU = mybir.AluOpType
ACT = mybir.ActivationFunctionType
AXIS = mybir.AxisListType

P = 128
PACK = 4
PER_WORD = 2
HALVES = PACK // PER_WORD
NODES = 1024
HID = 512
CLASSES = 256
GROUPS = 3
TILES = NODES // P
ROUND_TILES = (1, 2, 2, 2, 1)
ROUNDS = len(ROUND_TILES)
FIRST_TILE = tuple(sum(ROUND_TILES[:r]) for r in range(ROUNDS))
QUADRANTS = 4
assert sum(ROUND_TILES) == TILES

FLOPS = 2 * NODES * HID * HID + 2 * NODES * GROUPS * HID * CLASSES


def tile_gin_pc_kernel(
    tc, u1, W2_1_words, W2_1_scales, b2_1, h, h1, W_out_words, W_out_scales, b_out, out
):
    nc = tc.nc
    with ExitStack() as ctx:
        const = ctx.enter_context(tc.tile_pool(name="const", bufs=1))
        per_round = ctx.enter_context(tc.tile_pool(name="per_round", bufs=ROUNDS))
        per_tile = ctx.enter_context(tc.tile_pool(name="per_tile", bufs=TILES))
        scratch = ctx.enter_context(tc.tile_pool(name="scratch", bufs=2))
        word_banks = ctx.enter_context(tc.psum_pool(name="word_banks", bufs=4))
        h2_banks = ctx.enter_context(tc.psum_pool(name="h2_banks", bufs=2))
        logit_banks = ctx.enter_context(tc.psum_pool(name="logit_banks", bufs=2))
        ctx.enter_context(tc.manual_schedule())

        bias_rows = const.tile([P, HID + CLASSES], BF16)
        nc.vector.memset(bias_rows[:], 0.0)
        w21_plane = const.tile([P, HID], U8, align_bytes=64)
        nc.vector.memset(w21_plane[:].bitcast(I32), 0)
        ones = const.tile([P, P], BF16)
        nc.vector.memset(ones[:], 1.0)
        wout_planes = const.tile([P, CLASSES], U8, align_bytes=64)
        nc.vector.memset(wout_planes[:].bitcast(I32), 0)
        zero_col = const.tile([P, 1], F32)
        nc.vector.memset(zero_col[:], 0.0)

        one_col = const.tile([P, 1], F32)
        nc.scalar.activation(out=one_col[:], in_=zero_col[:], func=ACT.Exp)

        ident_f32 = const.tile([P, P], F32)
        make_identity(nc, ident_f32[:])

        def tiles_of(r):
            return slice(FIRST_TILE[r], FIRST_TILE[r] + ROUND_TILES[r])

        def load_round(x, r, tag):
            x_sb = per_round.tile([P, ROUND_TILES[r], HID], BF16, tag=tag)
            nc.sync.dma_start(
                out=x_sb[:], in_=x.rearrange("(p a) k -> p a k", a=TILES)[:, tiles_of(r), :]
            )
            return x_sb

        u1_sb, h_sb, h1_sb = {}, {}, {}
        u1_sb[0] = load_round(u1, 0, "u1_sb")
        nc.sync.dma_start(out=bias_rows[0:1, 0:HID], in_=b2_1.rearrange("(o n) -> o n", o=1))
        u1_sb[1] = load_round(u1, 1, "u1_sb")

        for quad in range(QUADRANTS):
            nc.sync.dma_start(
                out=w21_plane[32 * quad : 32 * quad + PACK, :].bitcast(I32),
                in_=W2_1_scales[0, PACK * quad : PACK * (quad + 1), :].bitcast(I32),
            )
        w21_words = const.tile([P, HID], U32, align_bytes=64)
        nc.sync.dma_start(
            out=w21_words[:].bitcast(I32),
            in_=W2_1_words[0].rearrange("p n t -> p (n t)").bitcast(I32),
        )

        for r in range(2, ROUNDS):
            u1_sb[r] = load_round(u1, r, "u1_sb")
        nc.sync.dma_start(out=bias_rows[0:1, HID:], in_=b_out.rearrange("(o n) -> o n", o=1))
        for r in range(0, 2):
            h_sb[r] = load_round(h, r, "h_sb")
            h1_sb[r] = load_round(h1, r, "h1_sb")

        for quad in range(QUADRANTS):
            nc.sync.dma_start(
                out=wout_planes[32 * quad : 32 * quad + PACK * GROUPS, :].bitcast(I32),
                in_=W_out_scales[:, PACK * quad : PACK * (quad + 1), :].bitcast(I32),
            )
        wout_words = const.tile([P, GROUPS, CLASSES], U32, align_bytes=64)
        nc.sync.dma_start(
            out=wout_words[:].bitcast(I32),
            in_=W_out_words.rearrange("g p n t -> p g (n t)").bitcast(I32),
        )
        for r in range(2, ROUNDS):
            h_sb[r] = load_round(h, r, "h_sb")
            h1_sb[r] = load_round(h1, r, "h1_sb")

        def transpose_words(r, word_cols, grouped_cols):
            words_t = word_banks.tile([P, ROUND_TILES[r], HALVES, P], F32)
            for a in range(ROUND_TILES[r]):
                for u in range(HALVES):
                    nc.tensor.transpose(words_t[:, a, u, :], word_cols(a, u), ident_f32[:])
            nc.scalar.copy(
                out=grouped_cols.bitcast(F32).rearrange(
                    "p (a w u) -> p a w u", a=ROUND_TILES[r], u=HALVES
                ),
                in_=words_t[:].rearrange("p a u w -> p a w u"),
            )

        def input_words(x_sb):
            return lambda a, u: x_sb[:, a, :].bitcast(F32)[:, u : HID // PER_WORD : HALVES]

        u1_grouped, u1_codes, u1_planes = {}, {}, {}
        cat_grouped, cat_codes, cat_planes = {}, {}, {}
        for r in range(ROUNDS):
            nodes = ROUND_TILES[r] * P
            u1_grouped[r] = per_round.tile(
                [P, nodes * PACK], BF16, align_bytes=64, name="u1_grouped", tag="u1_grouped"
            )
            u1_codes[r] = per_round.tile(
                [P, nodes], U32, align_bytes=64, name="u1_codes", tag="u1_codes"
            )
            u1_planes[r] = per_round.tile(
                [P, nodes], U8, align_bytes=64, name="u1_planes", tag="u1_planes"
            )
            cat_grouped[r] = per_round.tile(
                [P, GROUPS, nodes * PACK], BF16, align_bytes=64,
                name="cat_grouped", tag="cat_grouped",
            )
            cat_codes[r] = per_round.tile(
                [P, GROUPS, nodes], U32, align_bytes=64, name="cat_codes", tag="cat_codes"
            )
            cat_planes[r] = per_round.tile(
                [P, GROUPS, nodes], U8, align_bytes=64, name="cat_planes", tag="cat_planes"
            )

        def transpose_u1(r):
            transpose_words(r, input_words(u1_sb[r]), u1_grouped[r][:])

        def quantise_u1(r):
            nc.vector.quantize_mx(
                out=u1_codes[r][:].bitcast(FP8X4), scales=u1_planes[r][:], in_=u1_grouped[r][:]
            )

        def transpose_h_h1(r):
            transpose_words(r, input_words(h_sb[r]), cat_grouped[r][:, 0, :])
            transpose_words(r, input_words(h1_sb[r]), cat_grouped[r][:, 1, :])

        def quantise_h_h1(r):
            nc.vector.quantize_mx(
                out=cat_codes[r][:, 0:2, :].rearrange("p g w -> p (g w)").bitcast(FP8X4),
                scales=cat_planes[r][:, 0:2, :].rearrange("p g w -> p (g w)"),
                in_=cat_grouped[r][:, 0:2, :].rearrange("p g c -> p (g c)"),
            )

        by_half = "p (j u e) -> p u j e"
        h2_sorted = {}

        def first_matmul(r):
            for a in range(ROUND_TILES[r]):
                tile_nodes = slice(a * P, (a + 1) * P)
                h2_acc = h2_banks.tile([P, HID], F32, tag="h2_bank")
                nc.tensor.matmul_mx(
                    out=h2_acc[:],
                    lhsT=u1_codes[r][:, tile_nodes].bitcast(FP8X4),
                    lhsT_scale=u1_planes[r][:, tile_nodes],
                    rhs=w21_words[:].bitcast(FP8X4),
                    rhs_scale=w21_plane[:],
                    start=True,
                    stop=True,
                )
                h2_sorted[r, a] = per_tile.tile(
                    [P, HALVES, P, PER_WORD], BF16, name="h2_sorted", tag="h2_sorted"
                )
                nc.vector.tensor_tensor(
                    out=h2_sorted[r, a][:],
                    in0=h2_acc[:].rearrange(by_half, u=HALVES, e=PER_WORD),
                    in1=b2_sorted[:],
                    op=ALU.add,
                )

        def transpose_h2(r):
            transpose_words(
                r,
                lambda a, u: h2_sorted[r, a][:, u, :, :].rearrange("p j e -> p (j e)").bitcast(F32),
                cat_grouped[r][:, 2, :],
            )

        def quantise_h2(r):
            nc.vector.quantize_mx(
                out=cat_codes[r][:, 2, :].bitcast(FP8X4),
                scales=cat_planes[r][:, 2, :],
                in_=cat_grouped[r][:, 2, :],
            )

        logit_acc, logits = {}, {}
        neg_max = const.tile([P, TILES], F32)
        sums = const.tile([P, TILES], F32)

        def second_matmul(r):
            logit_acc[r] = logit_banks.tile(
                [P, ROUND_TILES[r], CLASSES], F32, name="logit_acc", tag="logit_acc"
            )
            for a in range(ROUND_TILES[r]):
                tile_nodes = slice(a * P, (a + 1) * P)
                for g in range(GROUPS):
                    nc.tensor.matmul_mx(
                        out=logit_acc[r][:, a, :],
                        lhsT=cat_codes[r][:, g, tile_nodes].bitcast(FP8X4),
                        lhsT_scale=cat_planes[r][:, g, tile_nodes],
                        rhs=wout_words[:, g, :].bitcast(FP8X4),
                        rhs_scale=wout_planes[PACK * g : P, :],
                        start=(g == 0),
                        stop=(g == GROUPS - 1),
                    )

        def logits_and_max(r):
            shape = [P, ROUND_TILES[r], CLASSES]
            logits[r] = per_round.tile(shape, F32, name="logits", tag="logits")
            nc.vector.tensor_tensor(
                out=logits[r][:],
                in0=logit_acc[r][:],
                in1=bout_all[:].unsqueeze(1).to_broadcast(shape),
                op=ALU.add,
            )
            nc.vector.tensor_reduce(
                out=neg_max[:, tiles_of(r)], in_=logits[r][:], axis=AXIS.X, op=ALU.max, negate=True
            )

        def exp_sums(r):
            for a in range(ROUND_TILES[r]):
                i = FIRST_TILE[r] + a
                exps = scratch.tile([P, CLASSES], F32)
                nc.scalar.activation(
                    out=exps[:],
                    in_=logits[r][:, a, :],
                    func=ACT.Exp,
                    bias=neg_max[:, i : i + 1],
                    scale=1.0,
                    accum_out=sums[:, i : i + 1],
                )

        transpose_u1(0)
        quantise_u1(0)

        b2_bank = h2_banks.tile([P, HID], F32, tag="h2_bank")
        nc.tensor.matmul(out=b2_bank[:], lhsT=ones[:], rhs=bias_rows[:, 0:HID], start=True, stop=True)
        b2_sorted = const.tile([P, HALVES, P, PER_WORD], F32)
        nc.vector.tensor_copy(out=b2_sorted[:], in_=b2_bank[:].rearrange(by_half, u=HALVES, e=PER_WORD))

        transpose_u1(1)
        quantise_u1(1)

        def if_round(stage, r):
            if 0 <= r < ROUNDS:
                stage(r)

        def step(i):
            if_round(quantise_h2, i - 2)
            if_round(first_matmul, i)
            if_round(second_matmul, i - 3)
            if_round(transpose_u1, i + 2)
            if_round(quantise_u1, i + 2)
            if_round(quantise_h_h1, i - 2)
            if_round(logits_and_max, i - 3)
            if_round(exp_sums, i - 4)
            if_round(transpose_h2, i - 1)
            if_round(transpose_h_h1, i - 1)

        step(0)
        step(1)
        bout_bank = logit_banks.tile([P, CLASSES], F32, tag="logit_acc")
        nc.tensor.matmul(
            out=bout_bank[:], lhsT=ones[:], rhs=bias_rows[:, HID:], start=True, stop=True
        )
        bout_all = const.tile([P, CLASSES], F32)
        nc.scalar.copy(out=bout_all[:], in_=bout_bank[:])
        for i in range(2, ROUNDS + 4):
            step(i)

        log_sums = const.tile([P, TILES], F32)
        nc.scalar.activation(out=log_sums[:], in_=sums[:], func=ACT.Ln)
        for r in range(ROUNDS):
            for a in range(ROUND_TILES[r]):
                i = FIRST_TILE[r] + a
                nc.vector.tensor_scalar(
                    out=logits[r][:, a, :],
                    in0=logits[r][:, a, :],
                    scalar1=neg_max[:, i : i + 1],
                    scalar2=log_sums[:, i : i + 1],
                    op0=ALU.add,
                    op1=ALU.subtract,
                )
            nc.sync.dma_start(
                out=out.rearrange("(p a) c -> p a c", a=TILES)[:, tiles_of(r), :], in_=logits[r][:]
            )
